import numpy as np
import ml_dtypes


def mxq(x, axis, fmt="e4m3"):
    dtype, down = {"e4m3": (ml_dtypes.float8_e4m3fn, 7), "e5m2": (ml_dtypes.float8_e5m2, 14)}[fmt]
    v = np.moveaxis(np.asarray(x, np.float32).astype(ml_dtypes.bfloat16).astype(np.float64), axis, -1)
    blocks = v.reshape(v.shape[:-1] + (-1, 32))
    amax = np.abs(blocks).max(-1, keepdims=True)
    byte = np.maximum(np.where(amax > 0, np.frexp(amax)[1] - 1 + 127, 0) - down, 1)
    scale = np.exp2(byte - 127.0)
    codes = (blocks / scale).astype(np.float32).astype(dtype).astype(np.float64)
    return np.moveaxis((codes * scale).reshape(v.shape), -1, axis)


WIDE = False


def mx_kscale(k):
    if not WIDE:
        return np.ones(k)
    levels = np.array([10, -10, 5, -5, 0])
    a = np.random.permutation(np.resize(levels, k // 512 * 4)).reshape(k // 512, 4)
    idx = np.arange(k)
    return np.exp2(a[idx // 512, idx % 128 // 32])


BF16 = ml_dtypes.bfloat16


def bf(x):
    return np.asarray(x, np.float32).astype(BF16)


def f64(x):
    return np.asarray(x).astype(np.float64)


B, L, C, BLOCK, WINDOW = 1, 2560, 512, 512, 2
NB = L // BLOCK


def setup_inputs():
    s = mx_kscale(C)
    return {"q": bf(np.random.standard_normal((B, L, C)) * s),
            "k": bf(np.random.standard_normal((B, L, C)) * 1.5 / s),
            "v": bf(np.random.standard_normal((B, L, C)) * 1.5)}


def reference(q, k, v):
    qq = mxq(f64(q), 2, "e4m3")
    kq = mxq(f64(k), 2, "e4m3")
    vf = f64(v)
    vq = mxq(vf, 1, "e4m3")
    block_mean = vf.reshape(B, NB, BLOCK, C).sum(2) / BLOCK
    res = np.zeros((B, L, C))
    for i in range(NB):
        lo, hi = max(i - WINDOW, 0), min(i + WINDOW + 1, NB)
        rows = slice(i * BLOCK, (i + 1) * BLOCK)
        keys = slice(lo * BLOCK, hi * BLOCK)
        sc = (qq[:, rows] @ kq[:, keys].transpose(0, 2, 1)) / np.sqrt(C)
        e = np.exp(sc - sc.max(1, keepdims=True))
        attn = e / e.sum(1, keepdims=True)
        near = mxq(attn, 2, "e4m3") @ vq[:, keys]
        far = block_mean[:, :lo].sum(1) + block_mean[:, hi:].sum(1)
        res[:, rows] = near + far[:, None, :]
    return res

@@ -1,0 +1,218 @@
+from contextlib import ExitStack
+import math
+
+import concourse.mybir as mybir
+from concourse.masks import make_identity
+
+F32 = mybir.dt.float32
+BF16 = mybir.dt.bfloat16
+U32 = mybir.dt.uint32
+U8 = mybir.dt.uint8
+FP8X4 = mybir.dt.float8_e4m3fn_x4
+ALU = mybir.AluOpType
+ACT = mybir.ActivationFunctionType
+AXIS_X = mybir.AxisListType.X
+
+P = 128
+PACK = 4
+L = 2560
+C = 512
+BLOCK = 512
+WINDOW = 2
+NB = L // BLOCK
+TILES = BLOCK // P
+SCALE = 1.0 / math.sqrt(C)
+
+NEAR_PAIRS = sum(min(i + WINDOW + 1, NB) - max(i - WINDOW, 0) for i in range(NB))
+FLOPS = NEAR_PAIRS * 2 * 2 * BLOCK * BLOCK * C
+
+
+def near_blocks(i):
+    return list(range(max(i - WINDOW, 0), min(i + WINDOW + 1, NB)))
+
+
+def tile_vectorizedsparseattention_pa_kernel(tc, q, k, v, out):
+    nc = tc.nc
+    q_blocks = q.flatten_outer_dims().rearrange("(b p r) c -> b p (r c)", p=P, r=TILES)
+    k_blocks = k.flatten_outer_dims().rearrange("(b p r) c -> b p (r c)", p=P, r=TILES)
+    v_blocks = v.flatten_outer_dims().rearrange("(b p r) c -> b p (r c)", p=P, r=TILES)
+    out_blocks = out.flatten_outer_dims().rearrange("(b p r) c -> b p (r c)", p=P, r=TILES)
+
+    with ExitStack() as ctx:
+        keep = ctx.enter_context(tc.tile_pool(name="keep", bufs=1))
+        stage = ctx.enter_context(tc.tile_pool(name="stage", bufs=2))
+        soft = ctx.enter_context(tc.tile_pool(name="soft", bufs=3))
+        small = ctx.enter_context(tc.tile_pool(name="small", bufs=8))
+        psum_work = ctx.enter_context(tc.psum_pool(name="psum_work", bufs=4))
+        psum_acc = ctx.enter_context(tc.psum_pool(name="psum_acc", bufs=1))
+
+        q_raw = keep.tile([P, NB, TILES * C], BF16)
+        k_raw = keep.tile([P, NB, TILES * C], BF16)
+        v_raw = keep.tile([P, NB, TILES * C], BF16)
+        q_codes = keep.tile([P, NB, BLOCK], U32, align_bytes=64)
+        k_codes = keep.tile([P, NB, BLOCK], U32, align_bytes=64)
+        v_codes = keep.tile([P, NB, C], U32, align_bytes=64)
+        q_scales = keep.tile([P, NB, BLOCK], U8, align_bytes=64)
+        k_scales = keep.tile([P, NB, BLOCK], U8, align_bytes=64)
+        v_scales = keep.tile([P, NB, C], U8, align_bytes=64)
+
+        nc.sync.dma_start(out=k_raw[:, 0, :], in_=k_blocks[0])
+        nc.sync.dma_start(out=q_raw[:, 0, :], in_=q_blocks[0])
+        for b in range(NB):
+            if b > 0:
+                nc.sync.dma_start(out=k_raw[:, b, :], in_=k_blocks[b])
+            nc.sync.dma_start(out=v_raw[:, b, :], in_=v_blocks[b])
+        for b in range(1, NB):
+            nc.sync.dma_start(out=q_raw[:, b, :], in_=q_blocks[b])
+
+        identity = keep.tile([P, P], F32)
+        make_identity(nc, identity[:])
+        ones = keep.tile([P, P], BF16)
+        nc.vector.memset(ones[:], 1.0)
+
+        def quantise_channels(raw, codes, scales):
+            words = raw.bitcast(F32)
+            grouped = stage.tile([P, BLOCK * PACK], BF16, align_bytes=64, name="grouped")
+            grouped_words = grouped[:].bitcast(F32)
+            for half in range(2):
+                flipped = psum_work.tile([P, 512], F32, tag="work", name="flipped")
+                for h in range(2):
+                    for u in range(2):
+                        first = (2 * half + h) * (C // 2) + u * P
+                        nc.tensor.transpose(
+                            flipped[:, (2 * h + u) * P : (2 * h + u + 1) * P],
+                            words[:, first : first + P],
+                            identity[:],
+                        )
+                dst = grouped_words[:, half * 512 : (half + 1) * 512].rearrange(
+                    "p (h r u) -> p h r u", h=2, u=2
+                )
+                src = flipped[:].rearrange("p (h u r) -> p h r u", h=2, u=2)
+                if half == 0:
+                    nc.scalar.copy(out=dst, in_=src)
+                else:
+                    nc.vector.tensor_copy(out=dst, in_=src)
+            nc.vector.quantize_mx(out=codes.bitcast(FP8X4), scales=scales, in_=grouped[:])
+
+        def regroup(dst, src):
+            nc.vector.tensor_copy(
+                out=dst.rearrange("p (c i t) -> p c t i", i=4, t=PACK),
+                in_=src.rearrange("p (t c i) -> p c t i", i=4, t=PACK),
+            )
+
+        def quantise_values(j):
+            grouped = stage.tile([P, C * PACK], BF16, align_bytes=64, name="grouped")
+            regroup(grouped[:], v_raw[:, j, :])
+            nc.vector.quantize_mx(
+                out=v_codes[:, j, :].bitcast(FP8X4), scales=v_scales[:, j, :], in_=grouped[:]
+            )
+
+        def scores_and_exp(i, j):
+            expd = soft.tile([P, TILES, BLOCK], F32, name="expd")
+            sums = small.tile([P, TILES], F32, name="sums")
+            for t in range(TILES):
+                keys = slice(t * P, (t + 1) * P)
+                s_ps = psum_work.tile([P, BLOCK], F32, tag="work", name="s_ps")
+                nc.tensor.matmul_mx(
+                    out=s_ps[:],
+                    lhsT=k_codes[:, j, keys].bitcast(FP8X4),
+                    lhsT_scale=k_scales[:, j, keys],
+                    rhs=q_codes[:, i, :].bitcast(FP8X4),
+                    rhs_scale=q_scales[:, i, :],
+                    start=True,
+                    stop=True,
+                )
+                top = small.tile([P, 1], F32, name="top")
+                nc.vector.tensor_reduce(out=top[:], in_=s_ps[:], axis=AXIS_X, op=ALU.max)
+                shift = small.tile([P, 1], F32, name="shift")
+                nc.vector.tensor_scalar_mul(out=shift[:], in0=top[:], scalar1=-SCALE)
+                nc.scalar.activation(
+                    out=expd[:, t, :],
+                    in_=s_ps[:],
+                    func=ACT.Exp,
+                    bias=shift[:],
+                    scale=SCALE,
+                    accum_out=sums[:, t : t + 1],
+                )
+            return expd, sums
+
+        def weights_times_values(j, expd, sums, acc, first, last):
+            inv = small.tile([P, TILES], F32, name="inv")
+            nc.vector.reciprocal(out=inv[:], in_=sums[:])
+            planes = soft.tile([P, TILES * BLOCK], BF16, name="planes")
+            for t in range(TILES):
+                nc.scalar.activation(
+                    out=planes[:, t * BLOCK : (t + 1) * BLOCK],
+                    in_=expd[:, t, :],
+                    func=ACT.Copy,
+                    scale=inv[:, t : t + 1],
+                )
+            grouped = soft.tile([P, BLOCK * PACK], BF16, align_bytes=64, name="a_grouped")
+            regroup(grouped[:], planes[:])
+            a_codes = soft.tile([P, BLOCK], U32, align_bytes=64, name="a_codes")
+            a_scales = soft.tile([P, BLOCK], U8, align_bytes=64, name="a_scales")
+            nc.vector.quantize_mx(out=a_codes[:].bitcast(FP8X4), scales=a_scales[:], in_=grouped[:])
+            for r in range(TILES):
+                queries = slice(r * P, (r + 1) * P)
+                nc.tensor.matmul_mx(
+                    out=acc[r][:],
+                    lhsT=a_codes[:, queries].bitcast(FP8X4),
+                    lhsT_scale=a_scales[:, queries],
+                    rhs=v_codes[:, j, :].bitcast(FP8X4),
+                    rhs_scale=v_scales[:, j, :],
+                    start=first,
+                    stop=last,
+                )
+
+        def far_term(i):
+            far = [j for j in range(NB) if j not in near_blocks(i)]
+            if not far:
+                return None
+            far_ps = psum_work.tile([P, C], F32, tag="work", name="far_ps")
+            steps = [(j, t) for j in far for t in range(TILES)]
+            for n, (j, t) in enumerate(steps):
+                nc.tensor.matmul(
+                    out=far_ps[:],
+                    lhsT=ones[:],
+                    rhs=v_raw[:, j, t * C : (t + 1) * C],
+                    start=(n == 0),
+                    stop=(n == len(steps) - 1),
+                )
+            far_sb = stage.tile([P, C], F32, name="far_sb")
+            nc.scalar.mul(out=far_sb[:], in_=far_ps[:], mul=1.0 / BLOCK)
+            return far_sb
+
+        def finish(i, acc):
+            far_sb = far_term(i)
+            result = stage.tile([P, TILES * C], F32, name="result")
+            for r in range(TILES):
+                dst = result[:, r * C : (r + 1) * C]
+                if far_sb is None:
+                    nc.scalar.copy(out=dst, in_=acc[r][:])
+                else:
+                    nc.vector.tensor_tensor(out=dst, in0=acc[r][:], in1=far_sb[:], op=ALU.add)
+            nc.sync.dma_start(out=out_blocks[i], in_=result[:])
+
+        def prepare(i, j):
+            if j == near_blocks(i)[0]:
+                quantise_channels(q_raw[:, i, :], q_codes[:, i, :], q_scales[:, i, :])
+            if i == max(j - WINDOW, 0):
+                quantise_channels(k_raw[:, j, :], k_codes[:, j, :], k_scales[:, j, :])
+                quantise_values(j)
+
+        pairs = [(i, j) for i in range(NB) for j in near_blocks(i)]
+        prepare(*pairs[0])
+        waiting = scores_and_exp(*pairs[0])
+        acc = None
+        for n, (i, j) in enumerate(pairs):
+            expd, sums = waiting
+            if n + 1 < len(pairs):
+                prepare(*pairs[n + 1])
+                waiting = scores_and_exp(*pairs[n + 1])
+            first = j == near_blocks(i)[0]
+            last = j == near_blocks(i)[-1]
+            if first:
+                acc = [psum_acc.tile([P, C], F32, name="acc%d" % r) for r in range(TILES)]
+            weights_times_values(j, expd, sums, acc, first, last)
+            if last:
+                finish(i, acc)

@@ -38,13 +38,30 @@ def tile_vectorizedsparseattention_pa_kernel(tc, q, k, v, out):
     v_blocks = v.flatten_outer_dims().rearrange("(b p r) c -> b p (r c)", p=P, r=TILES)
     out_blocks = out.flatten_outer_dims().rearrange("(b p r) c -> b p (r c)", p=P, r=TILES)
 
+    pairs = [(i, j) for i in range(NB) for j in near_blocks(i)]
+
+    def first_use_of_q(n):
+        i, j = pairs[n]
+        return j == near_blocks(i)[0]
+
+    def first_use_of_k_and_v(n):
+        i, j = pairs[n]
+        return i == max(j - WINDOW, 0)
+
+    def last_of_block(n):
+        i, j = pairs[n]
+        return j == near_blocks(i)[-1]
+
     with ExitStack() as ctx:
         keep = ctx.enter_context(tc.tile_pool(name="keep", bufs=1))
         stage = ctx.enter_context(tc.tile_pool(name="stage", bufs=2))
-        soft = ctx.enter_context(tc.tile_pool(name="soft", bufs=3))
-        small = ctx.enter_context(tc.tile_pool(name="small", bufs=8))
-        psum_work = ctx.enter_context(tc.psum_pool(name="psum_work", bufs=4))
+        soft = ctx.enter_context(tc.tile_pool(name="soft", bufs=2))
+        ahead = ctx.enter_context(tc.tile_pool(name="ahead", bufs=3))
+        small = ctx.enter_context(tc.tile_pool(name="small", bufs=4))
+        psum_score = ctx.enter_context(tc.psum_pool(name="psum_score", bufs=2))
+        psum_prep = ctx.enter_context(tc.psum_pool(name="psum_prep", bufs=2))
         psum_acc = ctx.enter_context(tc.psum_pool(name="psum_acc", bufs=1))
+        ctx.enter_context(tc.manual_schedule())
 
         q_raw = keep.tile([P, NB, TILES * C], BF16)
         k_raw = keep.tile([P, NB, TILES * C], BF16)
@@ -56,26 +73,35 @@ def tile_vectorizedsparseattention_pa_kernel(tc, q, k, v, out):
         k_scales = keep.tile([P, NB, BLOCK], U8, align_bytes=64)
         v_scales = keep.tile([P, NB, C], U8, align_bytes=64)
 
-        nc.sync.dma_start(out=k_raw[:, 0, :], in_=k_blocks[0])
-        nc.sync.dma_start(out=q_raw[:, 0, :], in_=q_blocks[0])
-        for b in range(NB):
-            if b > 0:
-                nc.sync.dma_start(out=k_raw[:, b, :], in_=k_blocks[b])
-            nc.sync.dma_start(out=v_raw[:, b, :], in_=v_blocks[b])
-        for b in range(1, NB):
-            nc.sync.dma_start(out=q_raw[:, b, :], in_=q_blocks[b])
+        for n in range(len(pairs) + 2):
+            if n < len(pairs) and first_use_of_k_and_v(n):
+                nc.sync.dma_start(out=k_raw[:, pairs[n][1], :], in_=k_blocks[pairs[n][1]])
+            if n < len(pairs) and first_use_of_q(n):
+                nc.sync.dma_start(out=q_raw[:, pairs[n][0], :], in_=q_blocks[pairs[n][0]])
+            if n >= 2 and first_use_of_k_and_v(n - 2):
+                nc.sync.dma_start(out=v_raw[:, pairs[n - 2][1], :], in_=v_blocks[pairs[n - 2][1]])
 
         identity = keep.tile([P, P], F32)
         make_identity(nc, identity[:])
         ones = keep.tile([P, P], BF16)
         nc.vector.memset(ones[:], 1.0)
 
-        def quantise_channels(raw, codes, scales):
-            words = raw.bitcast(F32)
-            grouped = stage.tile([P, BLOCK * PACK], BF16, align_bytes=64, name="grouped")
-            grouped_words = grouped[:].bitcast(F32)
+        tiles = {}
+
+        blocks = []
+        for n, (i, j) in enumerate(pairs):
+            if first_use_of_k_and_v(n):
+                blocks.append((k_raw[:, j, :], k_codes[:, j, :], k_scales[:, j, :]))
+            if first_use_of_q(n):
+                blocks.append((q_raw[:, i, :], q_codes[:, i, :], q_scales[:, i, :]))
+
+        def flip(b):
+            if not 0 <= b < len(blocks):
+                return
+            words = blocks[b][0].bitcast(F32)
             for half in range(2):
-                flipped = psum_work.tile([P, 512], F32, tag="work", name="flipped")
+                flipped = psum_prep.tile([P, 512], F32, tag="prep", name="flipped")
+                tiles["flipped", b, half] = flipped
                 for h in range(2):
                     for u in range(2):
                         first = (2 * half + h) * (C // 2) + u * P
@@ -84,135 +110,217 @@ def tile_vectorizedsparseattention_pa_kernel(tc, q, k, v, out):
                             words[:, first : first + P],
                             identity[:],
                         )
+
+        def collect(b):
+            if not 0 <= b < len(blocks):
+                return
+            grouped = ahead.tile([P, BLOCK * PACK], BF16, align_bytes=64, name="qk_grouped")
+            tiles["qk_grouped", b] = grouped
+            grouped_words = grouped[:].bitcast(F32)
+            for half in range(2):
                 dst = grouped_words[:, half * 512 : (half + 1) * 512].rearrange(
                     "p (h r u) -> p h r u", h=2, u=2
                 )
-                src = flipped[:].rearrange("p (h u r) -> p h r u", h=2, u=2)
+                src = tiles["flipped", b, half][:].rearrange("p (h u r) -> p h r u", h=2, u=2)
                 if half == 0:
                     nc.scalar.copy(out=dst, in_=src)
                 else:
                     nc.vector.tensor_copy(out=dst, in_=src)
-            nc.vector.quantize_mx(out=codes.bitcast(FP8X4), scales=scales, in_=grouped[:])
 
-        def regroup(dst, src):
-            nc.vector.tensor_copy(
-                out=dst.rearrange("p (c i t) -> p c t i", i=4, t=PACK),
-                in_=src.rearrange("p (t c i) -> p c t i", i=4, t=PACK),
-            )
-
-        def quantise_values(j):
-            grouped = stage.tile([P, C * PACK], BF16, align_bytes=64, name="grouped")
-            regroup(grouped[:], v_raw[:, j, :])
+        def quantise_channels(b):
+            if not 0 <= b < len(blocks):
+                return
+            raw, codes, scales = blocks[b]
             nc.vector.quantize_mx(
-                out=v_codes[:, j, :].bitcast(FP8X4), scales=v_scales[:, j, :], in_=grouped[:]
+                out=codes.bitcast(FP8X4), scales=scales, in_=tiles["qk_grouped", b][:]
             )
 
-        def scores_and_exp(i, j):
-            expd = soft.tile([P, TILES, BLOCK], F32, name="expd")
-            sums = small.tile([P, TILES], F32, name="sums")
-            for t in range(TILES):
-                keys = slice(t * P, (t + 1) * P)
-                s_ps = psum_work.tile([P, BLOCK], F32, tag="work", name="s_ps")
-                nc.tensor.matmul_mx(
-                    out=s_ps[:],
-                    lhsT=k_codes[:, j, keys].bitcast(FP8X4),
-                    lhsT_scale=k_scales[:, j, keys],
-                    rhs=q_codes[:, i, :].bitcast(FP8X4),
-                    rhs_scale=q_scales[:, i, :],
-                    start=True,
-                    stop=True,
-                )
-                top = small.tile([P, 1], F32, name="top")
-                nc.vector.tensor_reduce(out=top[:], in_=s_ps[:], axis=AXIS_X, op=ALU.max)
-                shift = small.tile([P, 1], F32, name="shift")
-                nc.vector.tensor_scalar_mul(out=shift[:], in0=top[:], scalar1=-SCALE)
-                nc.scalar.activation(
-                    out=expd[:, t, :],
-                    in_=s_ps[:],
-                    func=ACT.Exp,
-                    bias=shift[:],
-                    scale=SCALE,
-                    accum_out=sums[:, t : t + 1],
-                )
-            return expd, sums
+        def regroup_values(n):
+            if not 0 <= n < len(pairs) or not first_use_of_k_and_v(n):
+                return
+            tiles["v_grouped", n] = stage.tile([P, C * PACK], BF16, align_bytes=64, name="v_grouped")
+            nc.vector.tensor_copy(
+                out=tiles["v_grouped", n][:].rearrange("p (c i t) -> p c t i", i=4, t=PACK),
+                in_=v_raw[:, pairs[n][1], :].rearrange("p (t c i) -> p c t i", i=4, t=PACK),
+            )
 
-        def weights_times_values(j, expd, sums, acc, first, last):
-            inv = small.tile([P, TILES], F32, name="inv")
-            nc.vector.reciprocal(out=inv[:], in_=sums[:])
-            planes = soft.tile([P, TILES * BLOCK], BF16, name="planes")
+        def quantise_values(n):
+            if not 0 <= n < len(pairs) or not first_use_of_k_and_v(n):
+                return
+            j = pairs[n][1]
+            nc.vector.quantize_mx(
+                out=v_codes[:, j, :].bitcast(FP8X4),
+                scales=v_scales[:, j, :],
+                in_=tiles["v_grouped", n][:],
+            )
+
+        def score(n, t):
+            if not 0 <= n < len(pairs):
+                return
+            i, j = pairs[n]
+            keys = slice(t * P, (t + 1) * P)
+            s_ps = psum_score.tile([P, BLOCK], F32, name="s_ps")
+            tiles["s_ps", n, t] = s_ps
+            nc.tensor.matmul_mx(
+                out=s_ps[:],
+                lhsT=k_codes[:, j, keys].bitcast(FP8X4),
+                lhsT_scale=k_scales[:, j, keys],
+                rhs=q_codes[:, i, :].bitcast(FP8X4),
+                rhs_scale=q_scales[:, i, :],
+                start=True,
+                stop=True,
+            )
+
+        def take_max(n, t):
+            if not 0 <= n < len(pairs):
+                return
+            if t == 0:
+                tiles["neg", n] = ahead.tile([P, TILES, BLOCK], F32, name="neg")
+                tiles["shift", n] = small.tile([P, TILES], F32, name="shift")
+            nc.vector.tensor_scalar(
+                out=tiles["neg", n][:, t, :],
+                in0=tiles["s_ps", n, t][:],
+                scalar1=-SCALE,
+                scalar2=None,
+                op0=ALU.mult,
+                op1=ALU.min,
+                accum_out=tiles["shift", n][:, t : t + 1],
+            )
+
+        def exponent(n, t):
+            if not 0 <= n < len(pairs):
+                return
+            if t == 0:
+                tiles["expd", n] = soft.tile([P, TILES, BLOCK], F32, name="expd")
+                tiles["sums", n] = small.tile([P, TILES], F32, name="sums")
+            nc.scalar.activation(
+                out=tiles["expd", n][:, t, :],
+                in_=tiles["neg", n][:, t, :],
+                func=ACT.Exp,
+                bias=tiles["shift", n][:, t : t + 1],
+                scale=-1.0,
+                accum_out=tiles["sums", n][:, t : t + 1],
+            )
+
+        def invert(n):
+            if not 0 <= n < len(pairs):
+                return
+            tiles["inv", n] = small.tile([P, TILES], F32, name="inv")
+            nc.vector.reciprocal(out=tiles["inv", n][:], in_=tiles["sums", n][:])
+
+        def normalise(n):
+            if not 0 <= n < len(pairs):
+                return
+            tiles["planes", n] = soft.tile([P, TILES * BLOCK], BF16, name="planes")
             for t in range(TILES):
                 nc.scalar.activation(
-                    out=planes[:, t * BLOCK : (t + 1) * BLOCK],
-                    in_=expd[:, t, :],
+                    out=tiles["planes", n][:, t * BLOCK : (t + 1) * BLOCK],
+                    in_=tiles["expd", n][:, t, :],
                     func=ACT.Copy,
-                    scale=inv[:, t : t + 1],
+                    scale=tiles["inv", n][:, t : t + 1],
                 )
-            grouped = soft.tile([P, BLOCK * PACK], BF16, align_bytes=64, name="a_grouped")
-            regroup(grouped[:], planes[:])
-            a_codes = soft.tile([P, BLOCK], U32, align_bytes=64, name="a_codes")
-            a_scales = soft.tile([P, BLOCK], U8, align_bytes=64, name="a_scales")
-            nc.vector.quantize_mx(out=a_codes[:].bitcast(FP8X4), scales=a_scales[:], in_=grouped[:])
+
+        def regroup(n):
+            if not 0 <= n < len(pairs):
+                return
+            tiles["a_grouped", n] = soft.tile(
+                [P, BLOCK * PACK], BF16, align_bytes=64, name="a_grouped"
+            )
+            nc.gpsimd.tensor_scalar(
+                out=tiles["a_grouped", n][:].rearrange("p (w t) -> p w t", t=PACK),
+                in0=tiles["planes", n][:].rearrange("p (t w) -> p w t", t=PACK),
+                scalar1=1.0,
+                scalar2=0.0,
+                op0=ALU.mult,
+                op1=ALU.add,
+            )
+
+        def quantise(n):
+            if not 0 <= n < len(pairs):
+                return
+            tiles["a_codes", n] = soft.tile([P, BLOCK], U32, align_bytes=64, name="a_codes")
+            tiles["a_scales", n] = soft.tile([P, BLOCK], U8, align_bytes=64, name="a_scales")
+            nc.vector.quantize_mx(
+                out=tiles["a_codes", n][:].bitcast(FP8X4),
+                scales=tiles["a_scales", n][:],
+                in_=tiles["a_grouped", n][:],
+            )
+
+        def multiply(n):
+            if not 0 <= n < len(pairs):
+                return
+            i, j = pairs[n]
+            if first_use_of_q(n):
+                for r in range(TILES):
+                    tiles["acc", i, r] = psum_acc.tile([P, C], F32, name="acc%d" % r)
             for r in range(TILES):
                 queries = slice(r * P, (r + 1) * P)
                 nc.tensor.matmul_mx(
-                    out=acc[r][:],
-                    lhsT=a_codes[:, queries].bitcast(FP8X4),
-                    lhsT_scale=a_scales[:, queries],
+                    out=tiles["acc", i, r][:],
+                    lhsT=tiles["a_codes", n][:, queries].bitcast(FP8X4),
+                    lhsT_scale=tiles["a_scales", n][:, queries],
                     rhs=v_codes[:, j, :].bitcast(FP8X4),
                     rhs_scale=v_scales[:, j, :],
-                    start=first,
-                    stop=last,
+                    start=first_use_of_q(n),
+                    stop=last_of_block(n),
                 )
 
-        def far_term(i):
-            far = [j for j in range(NB) if j not in near_blocks(i)]
-            if not far:
-                return None
-            far_ps = psum_work.tile([P, C], F32, tag="work", name="far_ps")
-            steps = [(j, t) for j in far for t in range(TILES)]
-            for n, (j, t) in enumerate(steps):
+        def far_term(n):
+            if not 0 <= n < len(pairs) or not last_of_block(n):
+                return
+            i = pairs[n][0]
+            steps = [(j, t) for j in range(NB) if j not in near_blocks(i) for t in range(TILES)]
+            if not steps:
+                return
+            far_ps = psum_prep.tile([P, C], F32, tag="prep", name="far_ps")
+            for m, (j, t) in enumerate(steps):
                 nc.tensor.matmul(
                     out=far_ps[:],
                     lhsT=ones[:],
                     rhs=v_raw[:, j, t * C : (t + 1) * C],
-                    start=(n == 0),
-                    stop=(n == len(steps) - 1),
+                    start=(m == 0),
+                    stop=(m == len(steps) - 1),
                 )
-            far_sb = stage.tile([P, C], F32, name="far_sb")
-            nc.scalar.mul(out=far_sb[:], in_=far_ps[:], mul=1.0 / BLOCK)
-            return far_sb
+            tiles["far", i] = stage.tile([P, C], F32, name="far_sb")
+            nc.scalar.mul(out=tiles["far", i][:], in_=far_ps[:], mul=1.0 / BLOCK)
 
-        def finish(i, acc):
-            far_sb = far_term(i)
+        def finish(n):
+            if not 0 <= n < len(pairs) or not last_of_block(n):
+                return
+            i = pairs[n][0]
             result = stage.tile([P, TILES * C], F32, name="result")
             for r in range(TILES):
                 dst = result[:, r * C : (r + 1) * C]
-                if far_sb is None:
-                    nc.scalar.copy(out=dst, in_=acc[r][:])
+                if ("far", i) in tiles:
+                    nc.vector.tensor_tensor(
+                        out=dst, in0=tiles["acc", i, r][:], in1=tiles["far", i][:], op=ALU.add
+                    )
                 else:
-                    nc.vector.tensor_tensor(out=dst, in0=acc[r][:], in1=far_sb[:], op=ALU.add)
+                    nc.scalar.copy(out=dst, in_=tiles["acc", i, r][:])
             nc.sync.dma_start(out=out_blocks[i], in_=result[:])
 
-        def prepare(i, j):
-            if j == near_blocks(i)[0]:
-                quantise_channels(q_raw[:, i, :], q_codes[:, i, :], q_scales[:, i, :])
-            if i == max(j - WINDOW, 0):
-                quantise_channels(k_raw[:, j, :], k_codes[:, j, :], k_scales[:, j, :])
-                quantise_values(j)
-
-        pairs = [(i, j) for i in range(NB) for j in near_blocks(i)]
-        prepare(*pairs[0])
-        waiting = scores_and_exp(*pairs[0])
-        acc = None
-        for n, (i, j) in enumerate(pairs):
-            expd, sums = waiting
-            if n + 1 < len(pairs):
-                prepare(*pairs[n + 1])
-                waiting = scores_and_exp(*pairs[n + 1])
-            first = j == near_blocks(i)[0]
-            last = j == near_blocks(i)[-1]
-            if first:
-                acc = [psum_acc.tile([P, C], F32, name="acc%d" % r) for r in range(TILES)]
-            weights_times_values(j, expd, sums, acc, first, last)
-            if last:
-                finish(i, acc)
+        for n in range(-5, len(pairs) + 2):
+            invert(n)
+            exponent(n + 1, 0)
+            exponent(n + 1, 1)
+            take_max(n + 2, 0)
+            score(n + 2, 2)
+            take_max(n + 2, 1)
+            score(n + 2, 3)
+            flip(n + 5)
+            normalise(n)
+            regroup(n)
+            regroup_values(n + 1)
+            quantise(n - 1)
+            multiply(n - 1)
+            quantise_channels(n + 4)
+            quantise_values(n + 1)
+            take_max(n + 2, 2)
+            score(n + 3, 0)
+            take_max(n + 2, 3)
+            score(n + 3, 1)
+            exponent(n + 1, 2)
+            exponent(n + 1, 3)
+            finish(n - 1)
+            collect(n + 5)
+            far_term(n)

@@ -36,7 +36,7 @@ def tile_vectorizedsparseattention_pa_kernel(tc, q, k, v, out):
     q_blocks = q.flatten_outer_dims().rearrange("(b p r) c -> b p (r c)", p=P, r=TILES)
     k_blocks = k.flatten_outer_dims().rearrange("(b p r) c -> b p (r c)", p=P, r=TILES)
     v_blocks = v.flatten_outer_dims().rearrange("(b p r) c -> b p (r c)", p=P, r=TILES)
-    out_blocks = out.flatten_outer_dims().rearrange("(b p r) c -> b p (r c)", p=P, r=TILES)
+    out_tiles = out.flatten_outer_dims().rearrange("(b p r) c -> b r p c", p=P, r=TILES)
 
     pairs = [(i, j) for i in range(NB) for j in near_blocks(i)]
 
@@ -213,12 +213,15 @@ def tile_vectorizedsparseattention_pa_kernel(tc, q, k, v, out):
                 return
             tiles["planes", n] = soft.tile([P, TILES * BLOCK], BF16, name="planes")
             for t in range(TILES):
-                nc.scalar.activation(
-                    out=tiles["planes", n][:, t * BLOCK : (t + 1) * BLOCK],
-                    in_=tiles["expd", n][:, t, :],
-                    func=ACT.Copy,
-                    scale=tiles["inv", n][:, t : t + 1],
-                )
+                dst = tiles["planes", n][:, t * BLOCK : (t + 1) * BLOCK]
+                src = tiles["expd", n][:, t, :]
+                inv = tiles["inv", n][:, t : t + 1]
+                if t < TILES - 1:
+                    nc.scalar.activation(out=dst, in_=src, func=ACT.Copy, scale=inv)
+                else:
+                    nc.gpsimd.tensor_scalar(
+                        out=dst, in0=src, scalar1=inv, scalar2=0.0, op0=ALU.mult, op1=ALU.add
+                    )
 
         def regroup(n):
             if not 0 <= n < len(pairs):
@@ -296,8 +299,8 @@ def tile_vectorizedsparseattention_pa_kernel(tc, q, k, v, out):
                         out=dst, in0=tiles["acc", i, r][:], in1=tiles["far", i][:], op=ALU.add
                     )
                 else:
-                    nc.scalar.copy(out=dst, in_=tiles["acc", i, r][:])
-            nc.sync.dma_start(out=out_blocks[i], in_=result[:])
+                    nc.vector.tensor_copy(out=dst, in_=tiles["acc", i, r][:])
+                nc.sync.dma_start(out=out_tiles[i, r], in_=dst)
 
         for n in range(-5, len(pairs) + 2):
             invert(n)

@@ -11,7 +11,6 @@ U8 = mybir.dt.uint8
 FP8X4 = mybir.dt.float8_e4m3fn_x4
 ALU = mybir.AluOpType
 ACT = mybir.ActivationFunctionType
-AXIS_X = mybir.AxisListType.X
 
 P = 128
 PACK = 4
@@ -26,6 +25,20 @@ SCALE = 1.0 / math.sqrt(C)
 NEAR_PAIRS = sum(min(i + WINDOW + 1, NB) - max(i - WINDOW, 0) for i in range(NB))
 FLOPS = NEAR_PAIRS * 2 * 2 * BLOCK * BLOCK * C
 
+SB = 4
+FL = 4
+CL = -1
+FLIPS_SHARE = 1
+LEAD = 3
+CHUNKS = 1
+S_ORDER = 0
+QL = 1
+RCPOS = 1
+MXL = 2
+AG = 1
+RV_ENGINE = ['vector'] * 5
+SPLITFIN = 1
+
 
 def near_blocks(i):
     return list(range(max(i - WINDOW, 0), min(i + WINDOW + 1, NB)))
@@ -39,6 +52,7 @@ def tile_vectorizedsparseattention_pa_kernel(tc, q, k, v, out):
     out_tiles = out.flatten_outer_dims().rearrange("(b p r) c -> b r p c", p=P, r=TILES)
 
     pairs = [(i, j) for i in range(NB) for j in near_blocks(i)]
+    count = len(pairs)
 
     def first_use_of_q(n):
         i, j = pairs[n]
@@ -55,11 +69,12 @@ def tile_vectorizedsparseattention_pa_kernel(tc, q, k, v, out):
     with ExitStack() as ctx:
         keep = ctx.enter_context(tc.tile_pool(name="keep", bufs=1))
         stage = ctx.enter_context(tc.tile_pool(name="stage", bufs=2))
-        soft = ctx.enter_context(tc.tile_pool(name="soft", bufs=2))
+        soft = ctx.enter_context(tc.tile_pool(name="soft", bufs=3))
         ahead = ctx.enter_context(tc.tile_pool(name="ahead", bufs=3))
-        small = ctx.enter_context(tc.tile_pool(name="small", bufs=4))
-        psum_score = ctx.enter_context(tc.psum_pool(name="psum_score", bufs=2))
-        psum_prep = ctx.enter_context(tc.psum_pool(name="psum_prep", bufs=2))
+        single = ctx.enter_context(tc.tile_pool(name="single", bufs=AG))
+        small = ctx.enter_context(tc.tile_pool(name="small", bufs=6))
+        psum_bank = ctx.enter_context(tc.psum_pool(name="psum_bank", bufs=SB))
+        psum_aux = ctx.enter_context(tc.psum_pool(name="psum_aux", bufs=4 - SB)) if SB < 4 else psum_bank
         psum_acc = ctx.enter_context(tc.psum_pool(name="psum_acc", bufs=1))
         ctx.enter_context(tc.manual_schedule())
 
@@ -73,10 +88,10 @@ def tile_vectorizedsparseattention_pa_kernel(tc, q, k, v, out):
         k_scales = keep.tile([P, NB, BLOCK], U8, align_bytes=64)
         v_scales = keep.tile([P, NB, C], U8, align_bytes=64)
 
-        for n in range(len(pairs) + 2):
-            if n < len(pairs) and first_use_of_k_and_v(n):
+        for n in range(count + 2):
+            if n < count and first_use_of_k_and_v(n):
                 nc.sync.dma_start(out=k_raw[:, pairs[n][1], :], in_=k_blocks[pairs[n][1]])
-            if n < len(pairs) and first_use_of_q(n):
+            if n < count and first_use_of_q(n):
                 nc.sync.dma_start(out=q_raw[:, pairs[n][0], :], in_=q_blocks[pairs[n][0]])
             if n >= 2 and first_use_of_k_and_v(n - 2):
                 nc.sync.dma_start(out=v_raw[:, pairs[n - 2][1], :], in_=v_blocks[pairs[n - 2][1]])
@@ -91,61 +106,73 @@ def tile_vectorizedsparseattention_pa_kernel(tc, q, k, v, out):
         blocks = []
         for n, (i, j) in enumerate(pairs):
             if first_use_of_k_and_v(n):
-                blocks.append((k_raw[:, j, :], k_codes[:, j, :], k_scales[:, j, :]))
+                blocks.append((k_raw[:, j, :], k_codes[:, j, :], k_scales[:, j, :], n))
             if first_use_of_q(n):
-                blocks.append((q_raw[:, i, :], q_codes[:, i, :], q_scales[:, i, :]))
+                blocks.append((q_raw[:, i, :], q_codes[:, i, :], q_scales[:, i, :], n))
 
-        def flip(b):
-            if not 0 <= b < len(blocks):
-                return
+        def blocks_first_used_in(n):
+            return [b for b in range(len(blocks)) if blocks[b][3] == n]
+
+        def flip(b, half):
             words = blocks[b][0].bitcast(F32)
-            for half in range(2):
-                flipped = psum_prep.tile([P, 512], F32, tag="prep", name="flipped")
-                tiles["flipped", b, half] = flipped
-                for h in range(2):
-                    for u in range(2):
-                        first = (2 * half + h) * (C // 2) + u * P
-                        nc.tensor.transpose(
-                            flipped[:, (2 * h + u) * P : (2 * h + u + 1) * P],
-                            words[:, first : first + P],
-                            identity[:],
-                        )
+            flipped = (psum_bank if FLIPS_SHARE else psum_aux).tile([P, 512], F32, tag="bank", name="flipped")
+            tiles["flipped", b, half] = flipped
+            for h in range(2):
+                for u in range(2):
+                    first = (2 * half + h) * (C // 2) + u * P
+                    nc.tensor.transpose(
+                        flipped[:, (2 * h + u) * P : (2 * h + u + 1) * P],
+                        words[:, first : first + P],
+                        identity[:],
+                    )
 
-        def collect(b):
-            if not 0 <= b < len(blocks):
-                return
-            grouped = ahead.tile([P, BLOCK * PACK], BF16, align_bytes=64, name="qk_grouped")
-            tiles["qk_grouped", b] = grouped
-            grouped_words = grouped[:].bitcast(F32)
-            for half in range(2):
-                dst = grouped_words[:, half * 512 : (half + 1) * 512].rearrange(
-                    "p (h r u) -> p h r u", h=2, u=2
+        def collect(b, half, engine):
+            if half == 0:
+                tiles["qk_grouped", b] = ahead.tile(
+                    [P, BLOCK * PACK], BF16, align_bytes=64, name="qk_grouped"
                 )
-                src = tiles["flipped", b, half][:].rearrange("p (h u r) -> p h r u", h=2, u=2)
-                if half == 0:
-                    nc.scalar.copy(out=dst, in_=src)
-                else:
-                    nc.vector.tensor_copy(out=dst, in_=src)
+            grouped_words = tiles["qk_grouped", b][:].bitcast(F32)
+            dst = grouped_words[:, half * 512 : (half + 1) * 512].rearrange(
+                "p (h r u) -> p h r u", h=2, u=2
+            )
+            src = tiles["flipped", b, half][:].rearrange("p (h u r) -> p h r u", h=2, u=2)
+            if engine == "scalar":
+                nc.scalar.copy(out=dst, in_=src)
+            else:
+                nc.vector.tensor_copy(out=dst, in_=src)
 
         def quantise_channels(b):
-            if not 0 <= b < len(blocks):
-                return
-            raw, codes, scales = blocks[b]
+            raw, codes, scales, n = blocks[b]
             nc.vector.quantize_mx(
                 out=codes.bitcast(FP8X4), scales=scales, in_=tiles["qk_grouped", b][:]
             )
 
-        def regroup_values(n):
-            if not 0 <= n < len(pairs) or not first_use_of_k_and_v(n):
+        def regroup_values(n, engine):
+            if not 0 <= n < count or not first_use_of_k_and_v(n):
                 return
             tiles["v_grouped", n] = stage.tile([P, C * PACK], BF16, align_bytes=64, name="v_grouped")
-            nc.vector.tensor_copy(
-                out=tiles["v_grouped", n][:].rearrange("p (c i t) -> p c t i", i=4, t=PACK),
-                in_=v_raw[:, pairs[n][1], :].rearrange("p (t c i) -> p c t i", i=4, t=PACK),
-            )
+            if engine == "vector":
+                nc.vector.tensor_copy(
+                    out=tiles["v_grouped", n][:].rearrange("p (c i t) -> p c t i", i=4, t=PACK),
+                    in_=v_raw[:, pairs[n][1], :].rearrange("p (t c i) -> p c t i", i=4, t=PACK),
+                )
+            elif engine == "scalar":
+                nc.scalar.copy(
+                    out=tiles["v_grouped", n][:].rearrange("p (c t) -> p c t", t=PACK),
+                    in_=v_raw[:, pairs[n][1], :].rearrange("p (t c) -> p c t", t=PACK),
+                )
+            else:
+                nc.gpsimd.tensor_scalar(
+                    out=tiles["v_grouped", n][:].rearrange("p (c t) -> p c t", t=PACK),
+                    in0=v_raw[:, pairs[n][1], :].rearrange("p (t c) -> p c t", t=PACK),
+                    scalar1=1.0,
+                    scalar2=0.0,
+                    op0=ALU.mult,
+                    op1=ALU.add,
+                )
 
         def quantise_values(n):
-            if not 0 <= n < len(pairs) or not first_use_of_k_and_v(n):
+            if not 0 <= n < count or not first_use_of_k_and_v(n):
                 return
             j = pairs[n][1]
             nc.vector.quantize_mx(
@@ -155,11 +182,11 @@ def tile_vectorizedsparseattention_pa_kernel(tc, q, k, v, out):
             )
 
         def score(n, t):
-            if not 0 <= n < len(pairs):
+            if not 0 <= n < count:
                 return
             i, j = pairs[n]
             keys = slice(t * P, (t + 1) * P)
-            s_ps = psum_score.tile([P, BLOCK], F32, name="s_ps")
+            s_ps = psum_bank.tile([P, BLOCK], F32, tag="bank", name="s_ps")
             tiles["s_ps", n, t] = s_ps
             nc.tensor.matmul_mx(
                 out=s_ps[:],
@@ -172,7 +199,7 @@ def tile_vectorizedsparseattention_pa_kernel(tc, q, k, v, out):
             )
 
         def take_max(n, t):
-            if not 0 <= n < len(pairs):
+            if not 0 <= n < count:
                 return
             if t == 0:
                 tiles["neg", n] = ahead.tile([P, TILES, BLOCK], F32, name="neg")
@@ -188,10 +215,10 @@ def tile_vectorizedsparseattention_pa_kernel(tc, q, k, v, out):
             )
 
         def exponent(n, t):
-            if not 0 <= n < len(pairs):
+            if not 0 <= n < count:
                 return
             if t == 0:
-                tiles["expd", n] = soft.tile([P, TILES, BLOCK], F32, name="expd")
+                tiles["expd", n] = ahead.tile([P, TILES, BLOCK], F32, name="expd")
                 tiles["sums", n] = small.tile([P, TILES], F32, name="sums")
             nc.scalar.activation(
                 out=tiles["expd", n][:, t, :],
@@ -203,43 +230,53 @@ def tile_vectorizedsparseattention_pa_kernel(tc, q, k, v, out):
             )
 
         def invert(n):
-            if not 0 <= n < len(pairs):
+            if not 0 <= n < count:
                 return
             tiles["inv", n] = small.tile([P, TILES], F32, name="inv")
             nc.vector.reciprocal(out=tiles["inv", n][:], in_=tiles["sums", n][:])
 
-        def normalise(n):
-            if not 0 <= n < len(pairs):
+        def normalise(n, t, engine):
+            if not 0 <= n < count:
                 return
-            tiles["planes", n] = soft.tile([P, TILES * BLOCK], BF16, name="planes")
-            for t in range(TILES):
-                dst = tiles["planes", n][:, t * BLOCK : (t + 1) * BLOCK]
-                src = tiles["expd", n][:, t, :]
-                inv = tiles["inv", n][:, t : t + 1]
-                if t < TILES - 1:
-                    nc.scalar.activation(out=dst, in_=src, func=ACT.Copy, scale=inv)
-                else:
-                    nc.gpsimd.tensor_scalar(
-                        out=dst, in0=src, scalar1=inv, scalar2=0.0, op0=ALU.mult, op1=ALU.add
-                    )
+            if ("planes", n) not in tiles:
+                tiles["planes", n] = soft.tile([P, TILES * BLOCK], BF16, name="planes")
+            dst = tiles["planes", n][:, t * BLOCK : (t + 1) * BLOCK]
+            src = tiles["expd", n][:, t, :]
+            inv = tiles["inv", n][:, t : t + 1]
+            if engine == "scalar":
+                nc.scalar.activation(out=dst, in_=src, func=ACT.Copy, scale=inv)
+            elif engine == "gpsimd":
+                nc.gpsimd.tensor_scalar(
+                    out=dst, in0=src, scalar1=inv, scalar2=0.0, op0=ALU.mult, op1=ALU.add
+                )
+            else:
+                nc.vector.tensor_scalar(
+                    out=dst, in0=src, scalar1=inv, scalar2=None, op0=ALU.mult
+                )
 
         def regroup(n):
-            if not 0 <= n < len(pairs):
+            if not 0 <= n < count:
                 return
-            tiles["a_grouped", n] = soft.tile(
+            tiles["a_grouped", n] = single.tile(
                 [P, BLOCK * PACK], BF16, align_bytes=64, name="a_grouped"
             )
-            nc.gpsimd.tensor_scalar(
-                out=tiles["a_grouped", n][:].rearrange("p (w t) -> p w t", t=PACK),
-                in0=tiles["planes", n][:].rearrange("p (t w) -> p w t", t=PACK),
-                scalar1=1.0,
-                scalar2=0.0,
-                op0=ALU.mult,
-                op1=ALU.add,
-            )
+            width = BLOCK // CHUNKS
+            for c in range(CHUNKS):
+                nc.gpsimd.tensor_scalar(
+                    out=tiles["a_grouped", n][:].rearrange("p (w t) -> p w t", t=PACK)[
+                        :, c * width : (c + 1) * width, :
+                    ],
+                    in0=tiles["planes", n][:].rearrange("p (t w) -> p w t", t=PACK)[
+                        :, c * width : (c + 1) * width, :
+                    ],
+                    scalar1=1.0,
+                    scalar2=0.0,
+                    op0=ALU.mult,
+                    op1=ALU.add,
+                )
 
         def quantise(n):
-            if not 0 <= n < len(pairs):
+            if not 0 <= n < count:
                 return
             tiles["a_codes", n] = soft.tile([P, BLOCK], U32, align_bytes=64, name="a_codes")
             tiles["a_scales", n] = soft.tile([P, BLOCK], U8, align_bytes=64, name="a_scales")
@@ -250,7 +287,7 @@ def tile_vectorizedsparseattention_pa_kernel(tc, q, k, v, out):
             )
 
         def multiply(n):
-            if not 0 <= n < len(pairs):
+            if not 0 <= n < count:
                 return
             i, j = pairs[n]
             if first_use_of_q(n):
@@ -268,14 +305,16 @@ def tile_vectorizedsparseattention_pa_kernel(tc, q, k, v, out):
                     stop=last_of_block(n),
                 )
 
-        def far_term(n):
-            if not 0 <= n < len(pairs) or not last_of_block(n):
+        def far_steps(i):
+            return [(j, t) for j in range(NB) if j not in near_blocks(i) for t in range(TILES)]
+
+        def far_sum(n):
+            if not 0 <= n < count or not last_of_block(n) or not far_steps(pairs[n][0]):
                 return
             i = pairs[n][0]
-            steps = [(j, t) for j in range(NB) if j not in near_blocks(i) for t in range(TILES)]
-            if not steps:
-                return
-            far_ps = psum_prep.tile([P, C], F32, tag="prep", name="far_ps")
+            steps = far_steps(i)
+            far_ps = psum_aux.tile([P, C], F32, tag="bank", name="far_ps")
+            tiles["far_ps", i] = far_ps
             for m, (j, t) in enumerate(steps):
                 nc.tensor.matmul(
                     out=far_ps[:],
@@ -284,46 +323,67 @@ def tile_vectorizedsparseattention_pa_kernel(tc, q, k, v, out):
                     start=(m == 0),
                     stop=(m == len(steps) - 1),
                 )
-            tiles["far", i] = stage.tile([P, C], F32, name="far_sb")
-            nc.scalar.mul(out=tiles["far", i][:], in_=far_ps[:], mul=1.0 / BLOCK)
 
-        def finish(n):
-            if not 0 <= n < len(pairs) or not last_of_block(n):
+        def far_copy(n):
+            if not 0 <= n < count or not last_of_block(n) or not far_steps(pairs[n][0]):
                 return
             i = pairs[n][0]
-            result = stage.tile([P, TILES * C], F32, name="result")
-            for r in range(TILES):
-                dst = result[:, r * C : (r + 1) * C]
-                if ("far", i) in tiles:
-                    nc.vector.tensor_tensor(
-                        out=dst, in0=tiles["acc", i, r][:], in1=tiles["far", i][:], op=ALU.add
-                    )
-                else:
-                    nc.vector.tensor_copy(out=dst, in_=tiles["acc", i, r][:])
-                nc.sync.dma_start(out=out_tiles[i, r], in_=dst)
+            tiles["far", i] = stage.tile([P, C], F32, name="far_sb")
+            nc.scalar.mul(out=tiles["far", i][:], in_=tiles["far_ps", i][:], mul=1.0 / BLOCK)
 
-        for n in range(-5, len(pairs) + 2):
-            invert(n)
-            exponent(n + 1, 0)
-            exponent(n + 1, 1)
-            take_max(n + 2, 0)
-            score(n + 2, 2)
-            take_max(n + 2, 1)
-            score(n + 2, 3)
-            flip(n + 5)
-            normalise(n)
-            regroup(n)
-            regroup_values(n + 1)
+        def finish(n, r):
+            if not 0 <= n < count or not last_of_block(n):
+                return
+            i = pairs[n][0]
+            if r == 0:
+                tiles["result", i] = stage.tile([P, TILES * C], F32, name="result")
+            dst = tiles["result", i][:, r * C : (r + 1) * C]
+            if ("far", i) in tiles:
+                nc.vector.tensor_tensor(
+                    out=dst, in0=tiles["acc", i, r][:], in1=tiles["far", i][:], op=ALU.add
+                )
+            else:
+                nc.vector.tensor_copy(out=dst, in_=tiles["acc", i, r][:])
+            nc.sync.dma_start(out=out_tiles[i, r], in_=dst)
+
+        for n in range(-9, count + 4):
+            for b in blocks_first_used_in(n + MXL + 2):
+                quantise_channels(b)
+            quantise_values(n)
+            if 0 <= n + 1 < count and first_use_of_k_and_v(n + 1):
+                regroup_values(n + 1, RV_ENGINE[pairs[n + 1][1]])
             quantise(n - 1)
-            multiply(n - 1)
-            quantise_channels(n + 4)
-            quantise_values(n + 1)
-            take_max(n + 2, 2)
-            score(n + 3, 0)
-            take_max(n + 2, 3)
-            score(n + 3, 1)
-            exponent(n + 1, 2)
-            exponent(n + 1, 3)
-            finish(n - 1)
-            collect(n + 5)
-            far_term(n)
+            late = SPLITFIN and 0 <= n - 1 < count and first_use_of_q(n - 1) and n - 1 > 0
+            if not late:
+                multiply(n - 1)
+            regroup(n)
+            for t in range(TILES):
+                ahead_tile = (n + MXL) * TILES + t + LEAD
+                score(ahead_tile // TILES, ahead_tile % TILES)
+                take_max(n + MXL, t)
+                if t == RCPOS:
+                    invert(n + 1)
+                if SPLITFIN:
+                    if t >= 2:
+                        finish(n - 1, t - 2)
+                    else:
+                        finish(n - 2, t + 2)
+                else:
+                    finish(n - 1, t)
+            if late:
+                multiply(n - 1)
+            far_sum(n + 2)
+            for b in blocks_first_used_in(n + MXL + FL):
+                flip(b, 0)
+                flip(b, 1)
+            normalise(n + 1, TILES - 1, "gpsimd")
+            for b in blocks_first_used_in(n + MXL + FL + CL):
+                collect(b, 0, "scalar")
+                collect(b, 1, "vector" if n + MXL + FL + CL <= 0 else "scalar")
+            far_copy(n + 1)
+            exponent(n + 2, 0)
+            exponent(n + 2, 1)
+            for t in range(TILES - 1):
+                normalise(n + 1, t, "scalar")
+            exponent(n + 2, 2)
+            exponent(n + 2, 3)

@@ -35,7 +35,7 @@ S_ORDER = 0
 QL = 1
 RCPOS = 1
 MXL = 2
-AG = 1
+AG = 2
 RV_ENGINE = ['vector'] * 5
 SPLITFIN = 1
 

@@ -76,7 +76,16 @@ def tile_vectorizedsparseattention_pa_kernel(tc, q, k, v, out):
         psum_bank = ctx.enter_context(tc.psum_pool(name="psum_bank", bufs=SB))
         psum_aux = ctx.enter_context(tc.psum_pool(name="psum_aux", bufs=4 - SB)) if SB < 4 else psum_bank
         psum_acc = ctx.enter_context(tc.psum_pool(name="psum_acc", bufs=1))
-        ctx.enter_context(tc.manual_schedule())
+        ctx.enter_context(
+            tc.manual_schedule(
+                engines={
+                    mybir.EngineType.DVE,
+                    mybir.EngineType.Activation,
+                    mybir.EngineType.Pool,
+                    mybir.EngineType.SP,
+                }
+            )
+        )
 
         q_raw = keep.tile([P, NB, TILES * C], BF16)
         k_raw = keep.tile([P, NB, TILES * C], BF16)

@@ -26,6 +26,23 @@ NEAR_PAIRS = sum(min(i + WINDOW + 1, NB) - max(i - WINDOW, 0) for i in range(NB)
 FLOPS = NEAR_PAIRS * 2 * 2 * BLOCK * BLOCK * C
 
 SB = 4
+TAILV = 1
+NMVPOS = -1
+HEADF = 2
+ORDER = [0, 1, 2, 3, 4]
+PIECES = 0
+NM_LAST = ['svvv', 'ssvg', 'ssvg']
+LIGHT = [10, 15]
+NMT = 9
+QCLATE = 0
+PSC = 99
+FINS = 0
+S_LIST = 'E0 E1 N0 N1 N2 E2 E3'.split()
+GM = 4
+GK = 0
+NV = 0
+NVT = 1
+TAILN = 0
 FL = 4
 CL = -1
 FLIPS_SHARE = 1
@@ -49,9 +66,11 @@ def tile_vectorizedsparseattention_pa_kernel(tc, q, k, v, out):
     q_blocks = q.flatten_outer_dims().rearrange("(b p r) c -> b p (r c)", p=P, r=TILES)
     k_blocks = k.flatten_outer_dims().rearrange("(b p r) c -> b p (r c)", p=P, r=TILES)
     v_blocks = v.flatten_outer_dims().rearrange("(b p r) c -> b p (r c)", p=P, r=TILES)
+    q_pieces = q.flatten_outer_dims().rearrange("(b p r) c -> b r p c", p=P, r=TILES)
+    k_pieces = k.flatten_outer_dims().rearrange("(b p r) c -> b r p c", p=P, r=TILES)
     out_tiles = out.flatten_outer_dims().rearrange("(b p r) c -> b r p c", p=P, r=TILES)
 
-    pairs = [(i, j) for i in range(NB) for j in near_blocks(i)]
+    pairs = [(i, j) for i in ORDER for j in near_blocks(i)]
     count = len(pairs)
 
     def first_use_of_q(n):
@@ -59,8 +78,7 @@ def tile_vectorizedsparseattention_pa_kernel(tc, q, k, v, out):
         return j == near_blocks(i)[0]
 
     def first_use_of_k_and_v(n):
-        i, j = pairs[n]
-        return i == max(j - WINDOW, 0)
+        return pairs[n][1] not in [j for i, j in pairs[:n]]
 
     def last_of_block(n):
         i, j = pairs[n]
@@ -97,10 +115,15 @@ def tile_vectorizedsparseattention_pa_kernel(tc, q, k, v, out):
         k_scales = keep.tile([P, NB, BLOCK], U8, align_bytes=64)
         v_scales = keep.tile([P, NB, C], U8, align_bytes=64)
 
+        if PIECES:
+            for r in range(TILES):
+                nc.sync.dma_start(out=q_raw[:, pairs[0][0], r * C : (r + 1) * C], in_=q_pieces[pairs[0][0], r])
+            for r in range(TILES):
+                nc.sync.dma_start(out=k_raw[:, pairs[0][1], r * C : (r + 1) * C], in_=k_pieces[pairs[0][1], r])
         for n in range(count + 2):
-            if n < count and first_use_of_k_and_v(n):
+            if n < count and first_use_of_k_and_v(n) and not (PIECES and n == 0):
                 nc.sync.dma_start(out=k_raw[:, pairs[n][1], :], in_=k_blocks[pairs[n][1]])
-            if n < count and first_use_of_q(n):
+            if n < count and first_use_of_q(n) and not (PIECES and n == 0):
                 nc.sync.dma_start(out=q_raw[:, pairs[n][0], :], in_=q_blocks[pairs[n][0]])
             if n >= 2 and first_use_of_k_and_v(n - 2):
                 nc.sync.dma_start(out=v_raw[:, pairs[n - 2][1], :], in_=v_blocks[pairs[n - 2][1]])
@@ -120,7 +143,36 @@ def tile_vectorizedsparseattention_pa_kernel(tc, q, k, v, out):
                 blocks.append((q_raw[:, i, :], q_codes[:, i, :], q_scales[:, i, :], n))
 
         def blocks_first_used_in(n):
-            return [b for b in range(len(blocks)) if blocks[b][3] == n]
+            return [b for b in range(len(blocks)) if blocks[b][3] == n and not (PIECES and n == 0)]
+
+        def flip_piece(b, r):
+            words = blocks[b][0].bitcast(F32)
+            flipped = psum_bank.tile([P, 512], F32, tag="bank", name="flipped")
+            tiles["piece", b, r] = flipped
+            for u in range(2):
+                first = r * (C // 2) + u * P
+                nc.tensor.transpose(flipped[:, u * P : (u + 1) * P], words[:, first : first + P], identity[:])
+
+        def collect_piece(b, r, engine):
+            if r == 0:
+                tiles["qk_grouped", b] = ahead.tile(
+                    [P, BLOCK * PACK], BF16, align_bytes=64, name="qk_grouped"
+                )
+            grouped_words = tiles["qk_grouped", b][:].bitcast(F32)
+            dst = grouped_words[:, r * 256 : (r + 1) * 256].rearrange("p (m u) -> p m u", u=2)
+            src = tiles["piece", b, r][:, 0:256].rearrange("p (u m) -> p m u", u=2)
+            if engine == "scalar":
+                nc.scalar.copy(out=dst, in_=src)
+            else:
+                nc.vector.tensor_copy(out=dst, in_=src)
+
+        def quantise_piece(b, r):
+            raw, codes, scales, n = blocks[b]
+            nc.vector.quantize_mx(
+                out=codes[:, r * P : (r + 1) * P].bitcast(FP8X4),
+                scales=scales[:, r * P : (r + 1) * P],
+                in_=tiles["qk_grouped", b][:, r * P * PACK : (r + 1) * P * PACK],
+            )
 
         def flip(b, half):
             words = blocks[b][0].bitcast(F32)
@@ -266,6 +318,15 @@ def tile_vectorizedsparseattention_pa_kernel(tc, q, k, v, out):
         def regroup(n):
             if not 0 <= n < count:
                 return
+            if n >= count - TAILV:
+                tiles["a_grouped", n] = single.tile(
+                    [P, BLOCK * PACK], BF16, align_bytes=64, name="a_grouped"
+                )
+                nc.vector.tensor_copy(
+                    out=tiles["a_grouped", n][:].rearrange("p (w t) -> p w t", t=PACK),
+                    in_=tiles["planes", n][:].rearrange("p (t w) -> p w t", t=PACK),
+                )
+                return
             tiles["a_grouped", n] = single.tile(
                 [P, BLOCK * PACK], BF16, align_bytes=64, name="a_grouped"
             )
@@ -351,27 +412,62 @@ def tile_vectorizedsparseattention_pa_kernel(tc, q, k, v, out):
                 nc.vector.tensor_tensor(
                     out=dst, in0=tiles["acc", i, r][:], in1=tiles["far", i][:], op=ALU.add
                 )
+            elif FINS and r % 2 == 1:
+                nc.scalar.copy(out=dst, in_=tiles["acc", i, r][:])
             else:
                 nc.vector.tensor_copy(out=dst, in_=tiles["acc", i, r][:])
             nc.sync.dma_start(out=out_tiles[i, r], in_=dst)
 
+        if PIECES:
+            steps = [(1, r) for r in range(TILES)] + [(0, r) for r in range(TILES)]
+            for m, (b, r) in enumerate(steps):
+                flip_piece(b, r)
+                collect_piece(b, r, "scalar" if m % 2 == 0 else "vector")
+                if m >= 1:
+                    quantise_piece(steps[m - 1][0], steps[m - 1][1])
+                if m >= PSC:
+                    score(0, m - PSC)
+            quantise_piece(0, TILES - 1)
+        def engines_of(pair):
+            back = count - 1 - pair
+            if 0 <= back < len(NM_LAST):
+                return NM_LAST[back]
+            return "ssvg" if pair in LIGHT else "sssg"
+
         for n in range(-9, count + 4):
             for b in blocks_first_used_in(n + MXL + 2):
-                quantise_channels(b)
+                if not (QCLATE and blocks[b][3] <= HEADF):
+                    quantise_channels(b)
+                else:
+                    flip(b, 0)
+                    flip(b, 1)
             quantise_values(n)
             if 0 <= n + 1 < count and first_use_of_k_and_v(n + 1):
                 regroup_values(n + 1, RV_ENGINE[pairs[n + 1][1]])
+            if NMT == 9:
+                for tt in range(TILES):
+                    if engines_of(n)[tt] == "v":
+                        normalise(n, tt, "vector")
             quantise(n - 1)
             late = SPLITFIN and 0 <= n - 1 < count and first_use_of_q(n - 1) and n - 1 > 0
             if not late:
                 multiply(n - 1)
             regroup(n)
+            who = engines_of(n + 1)
             for t in range(TILES):
                 ahead_tile = (n + MXL) * TILES + t + LEAD
                 score(ahead_tile // TILES, ahead_tile % TILES)
                 take_max(n + MXL, t)
+                if QCLATE and t == 0:
+                    for b in blocks_first_used_in(n + MXL + 1):
+                        if blocks[b][3] <= HEADF:
+                            quantise_channels(b)
                 if t == RCPOS:
                     invert(n + 1)
+                if t == NMT:
+                    for tt in range(TILES):
+                        if who[tt] == "v":
+                            normalise(n + 1, tt, "vector")
                 if SPLITFIN:
                     if t >= 2:
                         finish(n - 1, t - 2)
@@ -383,16 +479,27 @@ def tile_vectorizedsparseattention_pa_kernel(tc, q, k, v, out):
                 multiply(n - 1)
             far_sum(n + 2)
             for b in blocks_first_used_in(n + MXL + FL):
-                flip(b, 0)
-                flip(b, 1)
-            normalise(n + 1, TILES - 1, "gpsimd")
+                if not (QCLATE and blocks[b][3] <= HEADF):
+                    flip(b, 0)
+                    flip(b, 1)
+            for t in range(TILES):
+                if who[t] == "g":
+                    normalise(n + 1, t, "gpsimd")
             for b in blocks_first_used_in(n + MXL + FL + CL):
-                collect(b, 0, "scalar")
-                collect(b, 1, "vector" if n + MXL + FL + CL <= 0 else "scalar")
+                if not (QCLATE and blocks[b][3] <= HEADF):
+                    collect(b, 0, "scalar")
+                    collect(b, 1, "vector" if n + MXL + FL + CL <= 0 else "scalar")
             far_copy(n + 1)
-            exponent(n + 2, 0)
-            exponent(n + 2, 1)
-            for t in range(TILES - 1):
-                normalise(n + 1, t, "scalar")
-            exponent(n + 2, 2)
-            exponent(n + 2, 3)
+            def scalar_normalise(t):
+                if who[t] == "s":
+                    normalise(n + 1, t, "scalar")
+
+            for step in S_LIST:
+                if step[0] == "E":
+                    exponent(n + 2, int(step[1]))
+                else:
+                    scalar_normalise(int(step[1]))
+            for b in blocks_first_used_in(n + MXL + 2):
+                if QCLATE and blocks[b][3] <= HEADF:
+                    collect(b, 0, "scalar")
+                    collect(b, 1, "scalar")

from contextlib import ExitStack
import math

import concourse.mybir as mybir
from concourse.masks import make_identity

F32 = mybir.dt.float32
BF16 = mybir.dt.bfloat16
U32 = mybir.dt.uint32
U8 = mybir.dt.uint8
FP8X4 = mybir.dt.float8_e4m3fn_x4
ALU = mybir.AluOpType
ACT = mybir.ActivationFunctionType

P = 128
PACK = 4
L = 2560
C = 512
BLOCK = 512
WINDOW = 2
NB = L // BLOCK
TILES = BLOCK // P
SCALE = 1.0 / math.sqrt(C)

NEAR_PAIRS = sum(min(i + WINDOW + 1, NB) - max(i - WINDOW, 0) for i in range(NB))
FLOPS = NEAR_PAIRS * 2 * 2 * BLOCK * BLOCK * C

SB = 4
TAILV = 1
NMVPOS = -1
HEADF = 2
ORDER = [0, 1, 2, 3, 4]
PIECES = 0
NM_LAST = ['svvv', 'ssvg', 'ssvg']
LIGHT = [10, 15]
NMT = 9
QCLATE = 0
PSC = 99
FINS = 0
S_LIST = 'E0 E1 N0 N1 N2 E2 E3'.split()
GM = 4
GK = 0
NV = 0
NVT = 1
TAILN = 0
FL = 4
CL = -1
FLIPS_SHARE = 1
LEAD = 3
CHUNKS = 1
S_ORDER = 0
QL = 1
RCPOS = 1
MXL = 2
AG = 2
RV_ENGINE = ['vector'] * 5
SPLITFIN = 1


def near_blocks(i):
    return list(range(max(i - WINDOW, 0), min(i + WINDOW + 1, NB)))


def tile_vectorizedsparseattention_pa_kernel(tc, q, k, v, out):
    nc = tc.nc
    q_blocks = q.flatten_outer_dims().rearrange("(b p r) c -> b p (r c)", p=P, r=TILES)
    k_blocks = k.flatten_outer_dims().rearrange("(b p r) c -> b p (r c)", p=P, r=TILES)
    v_blocks = v.flatten_outer_dims().rearrange("(b p r) c -> b p (r c)", p=P, r=TILES)
    q_pieces = q.flatten_outer_dims().rearrange("(b p r) c -> b r p c", p=P, r=TILES)
    k_pieces = k.flatten_outer_dims().rearrange("(b p r) c -> b r p c", p=P, r=TILES)
    out_tiles = out.flatten_outer_dims().rearrange("(b p r) c -> b r p c", p=P, r=TILES)

    pairs = [(i, j) for i in ORDER for j in near_blocks(i)]
    count = len(pairs)

    def first_use_of_q(n):
        i, j = pairs[n]
        return j == near_blocks(i)[0]

    def first_use_of_k_and_v(n):
        return pairs[n][1] not in [j for i, j in pairs[:n]]

    def last_of_block(n):
        i, j = pairs[n]
        return j == near_blocks(i)[-1]

    with ExitStack() as ctx:
        keep = ctx.enter_context(tc.tile_pool(name="keep", bufs=1))
        stage = ctx.enter_context(tc.tile_pool(name="stage", bufs=2))
        soft = ctx.enter_context(tc.tile_pool(name="soft", bufs=3))
        ahead = ctx.enter_context(tc.tile_pool(name="ahead", bufs=3))
        single = ctx.enter_context(tc.tile_pool(name="single", bufs=AG))
        small = ctx.enter_context(tc.tile_pool(name="small", bufs=6))
        psum_bank = ctx.enter_context(tc.psum_pool(name="psum_bank", bufs=SB))
        psum_aux = ctx.enter_context(tc.psum_pool(name="psum_aux", bufs=4 - SB)) if SB < 4 else psum_bank
        psum_acc = ctx.enter_context(tc.psum_pool(name="psum_acc", bufs=1))
        ctx.enter_context(
            tc.manual_schedule(
                engines={
                    mybir.EngineType.DVE,
                    mybir.EngineType.Activation,
                    mybir.EngineType.Pool,
                    mybir.EngineType.SP,
                }
            )
        )

        q_raw = keep.tile([P, NB, TILES * C], BF16)
        k_raw = keep.tile([P, NB, TILES * C], BF16)
        v_raw = keep.tile([P, NB, TILES * C], BF16)
        q_codes = keep.tile([P, NB, BLOCK], U32, align_bytes=64)
        k_codes = keep.tile([P, NB, BLOCK], U32, align_bytes=64)
        v_codes = keep.tile([P, NB, C], U32, align_bytes=64)
        q_scales = keep.tile([P, NB, BLOCK], U8, align_bytes=64)
        k_scales = keep.tile([P, NB, BLOCK], U8, align_bytes=64)
        v_scales = keep.tile([P, NB, C], U8, align_bytes=64)

        if PIECES:
            for r in range(TILES):
                nc.sync.dma_start(out=q_raw[:, pairs[0][0], r * C : (r + 1) * C], in_=q_pieces[pairs[0][0], r])
            for r in range(TILES):
                nc.sync.dma_start(out=k_raw[:, pairs[0][1], r * C : (r + 1) * C], in_=k_pieces[pairs[0][1], r])
        for n in range(count + 2):
            if n < count and first_use_of_k_and_v(n) and not (PIECES and n == 0):
                nc.sync.dma_start(out=k_raw[:, pairs[n][1], :], in_=k_blocks[pairs[n][1]])
            if n < count and first_use_of_q(n) and not (PIECES and n == 0):
                nc.sync.dma_start(out=q_raw[:, pairs[n][0], :], in_=q_blocks[pairs[n][0]])
            if n >= 2 and first_use_of_k_and_v(n - 2):
                nc.sync.dma_start(out=v_raw[:, pairs[n - 2][1], :], in_=v_blocks[pairs[n - 2][1]])

        identity = keep.tile([P, P], F32)
        make_identity(nc, identity[:])
        ones = keep.tile([P, P], BF16)
        nc.vector.memset(ones[:], 1.0)

        tiles = {}

        blocks = []
        for n, (i, j) in enumerate(pairs):
            if first_use_of_k_and_v(n):
                blocks.append((k_raw[:, j, :], k_codes[:, j, :], k_scales[:, j, :], n))
            if first_use_of_q(n):
                blocks.append((q_raw[:, i, :], q_codes[:, i, :], q_scales[:, i, :], n))

        def blocks_first_used_in(n):
            return [b for b in range(len(blocks)) if blocks[b][3] == n and not (PIECES and n == 0)]

        def flip_piece(b, r):
            words = blocks[b][0].bitcast(F32)
            flipped = psum_bank.tile([P, 512], F32, tag="bank", name="flipped")
            tiles["piece", b, r] = flipped
            for u in range(2):
                first = r * (C // 2) + u * P
                nc.tensor.transpose(flipped[:, u * P : (u + 1) * P], words[:, first : first + P], identity[:])

        def collect_piece(b, r, engine):
            if r == 0:
                tiles["qk_grouped", b] = ahead.tile(
                    [P, BLOCK * PACK], BF16, align_bytes=64, name="qk_grouped"
                )
            grouped_words = tiles["qk_grouped", b][:].bitcast(F32)
            dst = grouped_words[:, r * 256 : (r + 1) * 256].rearrange("p (m u) -> p m u", u=2)
            src = tiles["piece", b, r][:, 0:256].rearrange("p (u m) -> p m u", u=2)
            if engine == "scalar":
                nc.scalar.copy(out=dst, in_=src)
            else:
                nc.vector.tensor_copy(out=dst, in_=src)

        def quantise_piece(b, r):
            raw, codes, scales, n = blocks[b]
            nc.vector.quantize_mx(
                out=codes[:, r * P : (r + 1) * P].bitcast(FP8X4),
                scales=scales[:, r * P : (r + 1) * P],
                in_=tiles["qk_grouped", b][:, r * P * PACK : (r + 1) * P * PACK],
            )

        def flip(b, half):
            words = blocks[b][0].bitcast(F32)
            flipped = (psum_bank if FLIPS_SHARE else psum_aux).tile([P, 512], F32, tag="bank", name="flipped")
            tiles["flipped", b, half] = flipped
            for h in range(2):
                for u in range(2):
                    first = (2 * half + h) * (C // 2) + u * P
                    nc.tensor.transpose(
                        flipped[:, (2 * h + u) * P : (2 * h + u + 1) * P],
                        words[:, first : first + P],
                        identity[:],
                    )

        def collect(b, half, engine):
            if half == 0:
                tiles["qk_grouped", b] = ahead.tile(
                    [P, BLOCK * PACK], BF16, align_bytes=64, name="qk_grouped"
                )
            grouped_words = tiles["qk_grouped", b][:].bitcast(F32)
            dst = grouped_words[:, half * 512 : (half + 1) * 512].rearrange(
                "p (h r u) -> p h r u", h=2, u=2
            )
            src = tiles["flipped", b, half][:].rearrange("p (h u r) -> p h r u", h=2, u=2)
            if engine == "scalar":
                nc.scalar.copy(out=dst, in_=src)
            else:
                nc.vector.tensor_copy(out=dst, in_=src)

        def quantise_channels(b):
            raw, codes, scales, n = blocks[b]
            nc.vector.quantize_mx(
                out=codes.bitcast(FP8X4), scales=scales, in_=tiles["qk_grouped", b][:]
            )

        def regroup_values(n, engine):
            if not 0 <= n < count or not first_use_of_k_and_v(n):
                return
            tiles["v_grouped", n] = stage.tile([P, C * PACK], BF16, align_bytes=64, name="v_grouped")
            if engine == "vector":
                nc.vector.tensor_copy(
                    out=tiles["v_grouped", n][:].rearrange("p (c i t) -> p c t i", i=4, t=PACK),
                    in_=v_raw[:, pairs[n][1], :].rearrange("p (t c i) -> p c t i", i=4, t=PACK),
                )
            elif engine == "scalar":
                nc.scalar.copy(
                    out=tiles["v_grouped", n][:].rearrange("p (c t) -> p c t", t=PACK),
                    in_=v_raw[:, pairs[n][1], :].rearrange("p (t c) -> p c t", t=PACK),
                )
            else:
                nc.gpsimd.tensor_scalar(
                    out=tiles["v_grouped", n][:].rearrange("p (c t) -> p c t", t=PACK),
                    in0=v_raw[:, pairs[n][1], :].rearrange("p (t c) -> p c t", t=PACK),
                    scalar1=1.0,
                    scalar2=0.0,
                    op0=ALU.mult,
                    op1=ALU.add,
                )

        def quantise_values(n):
            if not 0 <= n < count or not first_use_of_k_and_v(n):
                return
            j = pairs[n][1]
            nc.vector.quantize_mx(
                out=v_codes[:, j, :].bitcast(FP8X4),
                scales=v_scales[:, j, :],
                in_=tiles["v_grouped", n][:],
            )

        def score(n, t):
            if not 0 <= n < count:
                return
            i, j = pairs[n]
            keys = slice(t * P, (t + 1) * P)
            s_ps = psum_bank.tile([P, BLOCK], F32, tag="bank", name="s_ps")
            tiles["s_ps", n, t] = s_ps
            nc.tensor.matmul_mx(
                out=s_ps[:],
                lhsT=k_codes[:, j, keys].bitcast(FP8X4),
                lhsT_scale=k_scales[:, j, keys],
                rhs=q_codes[:, i, :].bitcast(FP8X4),
                rhs_scale=q_scales[:, i, :],
                start=True,
                stop=True,
            )

        def take_max(n, t):
            if not 0 <= n < count:
                return
            if t == 0:
                tiles["neg", n] = ahead.tile([P, TILES, BLOCK], F32, name="neg")
                tiles["shift", n] = small.tile([P, TILES], F32, name="shift")
            nc.vector.tensor_scalar(
                out=tiles["neg", n][:, t, :],
                in0=tiles["s_ps", n, t][:],
                scalar1=-SCALE,
                scalar2=None,
                op0=ALU.mult,
                op1=ALU.min,
                accum_out=tiles["shift", n][:, t : t + 1],
            )

        def exponent(n, t):
            if not 0 <= n < count:
                return
            if t == 0:
                tiles["expd", n] = ahead.tile([P, TILES, BLOCK], F32, name="expd")
                tiles["sums", n] = small.tile([P, TILES], F32, name="sums")
            nc.scalar.activation(
                out=tiles["expd", n][:, t, :],
                in_=tiles["neg", n][:, t, :],
                func=ACT.Exp,
                bias=tiles["shift", n][:, t : t + 1],
                scale=-1.0,
                accum_out=tiles["sums", n][:, t : t + 1],
            )

        def invert(n):
            if not 0 <= n < count:
                return
            tiles["inv", n] = small.tile([P, TILES], F32, name="inv")
            nc.vector.reciprocal(out=tiles["inv", n][:], in_=tiles["sums", n][:])

        def normalise(n, t, engine):
            if not 0 <= n < count:
                return
            if ("planes", n) not in tiles:
                tiles["planes", n] = soft.tile([P, TILES * BLOCK], BF16, name="planes")
            dst = tiles["planes", n][:, t * BLOCK : (t + 1) * BLOCK]
            src = tiles["expd", n][:, t, :]
            inv = tiles["inv", n][:, t : t + 1]
            if engine == "scalar":
                nc.scalar.activation(out=dst, in_=src, func=ACT.Copy, scale=inv)
            elif engine == "gpsimd":
                nc.gpsimd.tensor_scalar(
                    out=dst, in0=src, scalar1=inv, scalar2=0.0, op0=ALU.mult, op1=ALU.add
                )
            else:
                nc.vector.tensor_scalar(
                    out=dst, in0=src, scalar1=inv, scalar2=None, op0=ALU.mult
                )

        def regroup(n):
            if not 0 <= n < count:
                return
            if n >= count - TAILV:
                tiles["a_grouped", n] = single.tile(
                    [P, BLOCK * PACK], BF16, align_bytes=64, name="a_grouped"
                )
                nc.vector.tensor_copy(
                    out=tiles["a_grouped", n][:].rearrange("p (w t) -> p w t", t=PACK),
                    in_=tiles["planes", n][:].rearrange("p (t w) -> p w t", t=PACK),
                )
                return
            tiles["a_grouped", n] = single.tile(
                [P, BLOCK * PACK], BF16, align_bytes=64, name="a_grouped"
            )
            width = BLOCK // CHUNKS
            for c in range(CHUNKS):
                nc.gpsimd.tensor_scalar(
                    out=tiles["a_grouped", n][:].rearrange("p (w t) -> p w t", t=PACK)[
                        :, c * width : (c + 1) * width, :
                    ],
                    in0=tiles["planes", n][:].rearrange("p (t w) -> p w t", t=PACK)[
                        :, c * width : (c + 1) * width, :
                    ],
                    scalar1=1.0,
                    scalar2=0.0,
                    op0=ALU.mult,
                    op1=ALU.add,
                )

        def quantise(n):
            if not 0 <= n < count:
                return
            tiles["a_codes", n] = soft.tile([P, BLOCK], U32, align_bytes=64, name="a_codes")
            tiles["a_scales", n] = soft.tile([P, BLOCK], U8, align_bytes=64, name="a_scales")
            nc.vector.quantize_mx(
                out=tiles["a_codes", n][:].bitcast(FP8X4),
                scales=tiles["a_scales", n][:],
                in_=tiles["a_grouped", n][:],
            )

        def multiply(n):
            if not 0 <= n < count:
                return
            i, j = pairs[n]
            if first_use_of_q(n):
                for r in range(TILES):
                    tiles["acc", i, r] = psum_acc.tile([P, C], F32, name="acc%d" % r)
            for r in range(TILES):
                queries = slice(r * P, (r + 1) * P)
                nc.tensor.matmul_mx(
                    out=tiles["acc", i, r][:],
                    lhsT=tiles["a_codes", n][:, queries].bitcast(FP8X4),
                    lhsT_scale=tiles["a_scales", n][:, queries],
                    rhs=v_codes[:, j, :].bitcast(FP8X4),
                    rhs_scale=v_scales[:, j, :],
                    start=first_use_of_q(n),
                    stop=last_of_block(n),
                )

        def far_steps(i):
            return [(j, t) for j in range(NB) if j not in near_blocks(i) for t in range(TILES)]

        def far_sum(n):
            if not 0 <= n < count or not last_of_block(n) or not far_steps(pairs[n][0]):
                return
            i = pairs[n][0]
            steps = far_steps(i)
            far_ps = psum_aux.tile([P, C], F32, tag="bank", name="far_ps")
            tiles["far_ps", i] = far_ps
            for m, (j, t) in enumerate(steps):
                nc.tensor.matmul(
                    out=far_ps[:],
                    lhsT=ones[:],
                    rhs=v_raw[:, j, t * C : (t + 1) * C],
                    start=(m == 0),
                    stop=(m == len(steps) - 1),
                )

        def far_copy(n):
            if not 0 <= n < count or not last_of_block(n) or not far_steps(pairs[n][0]):
                return
            i = pairs[n][0]
            tiles["far", i] = stage.tile([P, C], F32, name="far_sb")
            nc.scalar.mul(out=tiles["far", i][:], in_=tiles["far_ps", i][:], mul=1.0 / BLOCK)

        def finish(n, r):
            if not 0 <= n < count or not last_of_block(n):
                return
            i = pairs[n][0]
            if r == 0:
                tiles["result", i] = stage.tile([P, TILES * C], F32, name="result")
            dst = tiles["result", i][:, r * C : (r + 1) * C]
            if ("far", i) in tiles:
                nc.vector.tensor_tensor(
                    out=dst, in0=tiles["acc", i, r][:], in1=tiles["far", i][:], op=ALU.add
                )
            elif FINS and r % 2 == 1:
                nc.scalar.copy(out=dst, in_=tiles["acc", i, r][:])
            else:
                nc.vector.tensor_copy(out=dst, in_=tiles["acc", i, r][:])
            nc.sync.dma_start(out=out_tiles[i, r], in_=dst)

        if PIECES:
            steps = [(1, r) for r in range(TILES)] + [(0, r) for r in range(TILES)]
            for m, (b, r) in enumerate(steps):
                flip_piece(b, r)
                collect_piece(b, r, "scalar" if m % 2 == 0 else "vector")
                if m >= 1:
                    quantise_piece(steps[m - 1][0], steps[m - 1][1])
                if m >= PSC:
                    score(0, m - PSC)
            quantise_piece(0, TILES - 1)
        def engines_of(pair):
            back = count - 1 - pair
            if 0 <= back < len(NM_LAST):
                return NM_LAST[back]
            return "ssvg" if pair in LIGHT else "sssg"

        for n in range(-9, count + 4):
            for b in blocks_first_used_in(n + MXL + 2):
                if not (QCLATE and blocks[b][3] <= HEADF):
                    quantise_channels(b)
                else:
                    flip(b, 0)
                    flip(b, 1)
            quantise_values(n)
            if 0 <= n + 1 < count and first_use_of_k_and_v(n + 1):
                regroup_values(n + 1, RV_ENGINE[pairs[n + 1][1]])
            if NMT == 9:
                for tt in range(TILES):
                    if engines_of(n)[tt] == "v":
                        normalise(n, tt, "vector")
            quantise(n - 1)
            late = SPLITFIN and 0 <= n - 1 < count and first_use_of_q(n - 1) and n - 1 > 0
            if not late:
                multiply(n - 1)
            regroup(n)
            who = engines_of(n + 1)
            for t in range(TILES):
                ahead_tile = (n + MXL) * TILES + t + LEAD
                score(ahead_tile // TILES, ahead_tile % TILES)
                take_max(n + MXL, t)
                if QCLATE and t == 0:
                    for b in blocks_first_used_in(n + MXL + 1):
                        if blocks[b][3] <= HEADF:
                            quantise_channels(b)
                if t == RCPOS:
                    invert(n + 1)
                if t == NMT:
                    for tt in range(TILES):
                        if who[tt] == "v":
                            normalise(n + 1, tt, "vector")
                if SPLITFIN:
                    if t >= 2:
                        finish(n - 1, t - 2)
                    else:
                        finish(n - 2, t + 2)
                else:
                    finish(n - 1, t)
            if late:
                multiply(n - 1)
            far_sum(n + 2)
            for b in blocks_first_used_in(n + MXL + FL):
                if not (QCLATE and blocks[b][3] <= HEADF):
                    flip(b, 0)
                    flip(b, 1)
            for t in range(TILES):
                if who[t] == "g":
                    normalise(n + 1, t, "gpsimd")
            for b in blocks_first_used_in(n + MXL + FL + CL):
                if not (QCLATE and blocks[b][3] <= HEADF):
                    collect(b, 0, "scalar")
                    collect(b, 1, "vector" if n + MXL + FL + CL <= 0 else "scalar")
            far_copy(n + 1)
            def scalar_normalise(t):
                if who[t] == "s":
                    normalise(n + 1, t, "scalar")

            for step in S_LIST:
                if step[0] == "E":
                    exponent(n + 2, int(step[1]))
                else:
                    scalar_normalise(int(step[1]))
            for b in blocks_first_used_in(n + MXL + 2):
                if QCLATE and blocks[b][3] <= HEADF:
                    collect(b, 0, "scalar")
                    collect(b, 1, "scalar")
